import numpy as np
import ml_dtypes

BF16 = ml_dtypes.bfloat16


def bf(x):
    return np.asarray(x, np.float32).astype(BF16)


def f32(x):
    return np.asarray(x, np.float32)


def f64(x):
    return np.asarray(x).astype(np.float64)


def striped(idx):
    return np.tile(idx.reshape(-1, 16).T, (8, 1))


C, S, N, NA, R = 128, 512, 128, 4, 32


def setup_inputs():
    return {"base": f32(np.random.standard_normal((C, S))), "x": bf(np.random.standard_normal((C, N))), "wka": bf(np.random.standard_normal((C, C + NA * R)) / np.sqrt(C)), "wb": bf(np.random.standard_normal((NA * R, C)) / np.sqrt(R)), "offs": striped(np.random.permutation(S)[:N])}


def reference(base, x, wka, wb, offs):
    idx = offs[:16].T.reshape(-1)
    z = f64(wka).T @ f64(x)
    own = (np.arange(NA * R)[:, None] // R) == (np.arange(N)[None, :] // (N // NA))
    d = f64(wb).T @ (z[C:] * own)
    out = f64(base).copy()
    out[:, idx] = z[:C] + d
    return out

@@ -1,0 +1,54 @@
+import concourse.masks as masks
+import concourse.mybir as mybir
+
+BF16, F32, U16 = mybir.dt.bfloat16, mybir.dt.float32, mybir.dt.uint16
+
+C = 128
+S = 512
+N = 128
+RANK = 32
+Q = 128
+
+FLOPS = 2 * C * C * N + 2 * C * Q * N + 2 * RANK * C * N
+
+
+def tile_llamaattentionwithlora_s_kernel(tc, base, x, wka, wb, offs, out):
+    nc = tc.nc
+    with (
+        tc.tile_pool(name="held", bufs=1) as held,
+        tc.psum_pool(name="psum", bufs=1) as psum,
+    ):
+        tokens = held.tile([C, N], BF16, name="tokens")
+        nc.sync.dma_start(tokens[:], x)
+        down = held.tile([C, C + Q], BF16, name="down")
+        nc.scalar.dma_start(down[:], wka)
+        offsets = held.tile([C, N // 16], U16, name="offsets")
+        nc.sync.dma_start(offsets[:], offs)
+        up = held.tile([Q, C], BF16, name="up")
+        nc.scalar.dma_start(up[:], wb)
+        cache = held.tile([C, S], F32, name="cache")
+        nc.sync.dma_start(cache[:], base)
+
+        own = held.tile([Q, N], F32, name="own")
+        masks.make_block_diagonal(nc, own[:], RANK)
+
+        u_psum = psum.tile([Q, N], F32, name="u_psum")
+        nc.tensor.matmul(u_psum[:], down[:, C : C + Q], tokens[:], start=True, stop=True)
+        y_psum = psum.tile([C, N], F32, name="y_psum")
+        nc.tensor.matmul(y_psum[:], down[:, 0:C], tokens[:], start=True, stop=True)
+
+        u_own = held.tile([Q, N], BF16, name="u_own")
+        nc.vector.tensor_tensor(u_own[:], u_psum[:], own[:], mybir.AluOpType.mult)
+
+        y = held.tile([C, N], F32, name="y")
+        nc.scalar.copy(y[:], y_psum[:])
+
+        d_psum = psum.tile([C, N], F32, name="d_psum")
+        nc.tensor.matmul(d_psum[:], up[:], u_own[:], start=True, stop=True)
+
+        d = held.tile([C, N], F32, name="d")
+        nc.vector.tensor_copy(d[:], d_psum[:])
+
+        nc.vector.tensor_tensor(cache[:].indirect(offsets[:]), y[:], d[:], mybir.AluOpType.add)
+
+        nc.sync.dma_start(out, cache[:])

@@ -1,4 +1,3 @@
-import concourse.masks as masks
 import concourse.mybir as mybir
 
 BF16, F32, U16 = mybir.dt.bfloat16, mybir.dt.float32, mybir.dt.uint16
@@ -7,7 +6,8 @@ C = 128
 S = 512
 N = 128
 RANK = 32
-Q = 128
+ADAPTERS = 4
+Q = ADAPTERS * RANK
 
 FLOPS = 2 * C * C * N + 2 * C * Q * N + 2 * RANK * C * N
 
@@ -30,7 +30,10 @@ def tile_llamaattentionwithlora_s_kernel(tc, base, x, wka, wb, offs, out):
         nc.sync.dma_start(cache[:], base)
 
         own = held.tile([Q, N], F32, name="own")
-        masks.make_block_diagonal(nc, own[:], RANK)
+        nc.vector.memset(own[:], 0.0)
+        for a in range(ADAPTERS):
+            block = slice(a * RANK, (a + 1) * RANK)
+            nc.vector.memset(own[block, block], 1.0)
 
         u_psum = psum.tile([Q, N], F32, name="u_psum")
         nc.tensor.matmul(u_psum[:], down[:, C : C + Q], tokens[:], start=True, stop=True)

@@ -54,4 +54,6 @@ def tile_llamaattentionwithlora_s_kernel(tc, base, x, wka, wb, offs, out):
 
         nc.vector.tensor_tensor(cache[:].indirect(offsets[:]), y[:], d[:], mybir.AluOpType.add)
 
-        nc.sync.dma_start(out, cache[:])
+        half = C // 2
+        nc.sync.dma_start(out[0:half, :], cache[0:half, :])
+        nc.scalar.dma_start(out[half:C, :], cache[half:C, :])

@@ -43,17 +43,14 @@ def tile_llamaattentionwithlora_s_kernel(tc, base, x, wka, wb, offs, out):
         u_own = held.tile([Q, N], BF16, name="u_own")
         nc.vector.tensor_tensor(u_own[:], u_psum[:], own[:], mybir.AluOpType.mult)
 
-        y = held.tile([C, N], F32, name="y")
-        nc.scalar.copy(y[:], y_psum[:])
-
         d_psum = psum.tile([C, N], F32, name="d_psum")
         nc.tensor.matmul(d_psum[:], up[:], u_own[:], start=True, stop=True)
 
+        y = held.tile([C, N], F32, name="y")
+        nc.vector.tensor_copy(y[:], y_psum[:])
         d = held.tile([C, N], F32, name="d")
         nc.vector.tensor_copy(d[:], d_psum[:])
 
         nc.vector.tensor_tensor(cache[:].indirect(offsets[:]), y[:], d[:], mybir.AluOpType.add)
 
-        half = C // 2
-        nc.sync.dma_start(out[0:half, :], cache[0:half, :])
-        nc.scalar.dma_start(out[half:C, :], cache[half:C, :])
+        nc.sync.dma_start(out, cache[:])

@@ -18,14 +18,14 @@ def tile_llamaattentionwithlora_s_kernel(tc, base, x, wka, wb, offs, out):
         tc.tile_pool(name="held", bufs=1) as held,
         tc.psum_pool(name="psum", bufs=1) as psum,
     ):
+        down = held.tile([C, C + Q], BF16, name="down")
+        nc.sync.dma_start(down[:], wka)
         tokens = held.tile([C, N], BF16, name="tokens")
         nc.sync.dma_start(tokens[:], x)
-        down = held.tile([C, C + Q], BF16, name="down")
-        nc.scalar.dma_start(down[:], wka)
+        up = held.tile([Q, C], BF16, name="up")
+        nc.sync.dma_start(up[:], wb)
         offsets = held.tile([C, N // 16], U16, name="offsets")
         nc.sync.dma_start(offsets[:], offs)
-        up = held.tile([Q, C], BF16, name="up")
-        nc.scalar.dma_start(up[:], wb)
         cache = held.tile([C, S], F32, name="cache")
         nc.sync.dma_start(cache[:], base)
 

@@ -18,24 +18,24 @@ def tile_llamaattentionwithlora_s_kernel(tc, base, x, wka, wb, offs, out):
         tc.tile_pool(name="held", bufs=1) as held,
         tc.psum_pool(name="psum", bufs=1) as psum,
     ):
-        down = held.tile([C, C + Q], BF16, name="down")
-        nc.sync.dma_start(down[:], wka)
         tokens = held.tile([C, N], BF16, name="tokens")
         nc.sync.dma_start(tokens[:], x)
-        up = held.tile([Q, C], BF16, name="up")
-        nc.sync.dma_start(up[:], wb)
+        down = held.tile([C, C + Q], BF16, name="down")
+        nc.scalar.dma_start(down[:], wka)
         offsets = held.tile([C, N // 16], U16, name="offsets")
         nc.sync.dma_start(offsets[:], offs)
+        up = held.tile([Q, C], BF16, name="up")
+        nc.scalar.dma_start(up[:], wb)
         cache = held.tile([C, S], F32, name="cache")
         nc.sync.dma_start(cache[:], base)
 
-        own = held.tile([Q, N], F32, name="own")
+        own = held.tile([Q, N], BF16, name="own")
         nc.vector.memset(own[:], 0.0)
         for a in range(ADAPTERS):
             block = slice(a * RANK, (a + 1) * RANK)
             nc.vector.memset(own[block, block], 1.0)
 
-        u_psum = psum.tile([Q, N], F32, name="u_psum")
+        u_psum = psum.tile([Q, N], BF16, name="u_psum")
         nc.tensor.matmul(u_psum[:], down[:, C : C + Q], tokens[:], start=True, stop=True)
         y_psum = psum.tile([C, N], F32, name="y_psum")
         nc.tensor.matmul(y_psum[:], down[:, 0:C], tokens[:], start=True, stop=True)

@@ -8,6 +8,7 @@ N = 128
 RANK = 32
 ADAPTERS = 4
 Q = ADAPTERS * RANK
+HALF = N // 2
 
 FLOPS = 2 * C * C * N + 2 * C * Q * N + 2 * RANK * C * N
 
@@ -35,21 +36,25 @@ def tile_llamaattentionwithlora_s_kernel(tc, base, x, wka, wb, offs, out):
             block = slice(a * RANK, (a + 1) * RANK)
             nc.vector.memset(own[block, block], 1.0)
 
-        u_psum = psum.tile([Q, N], BF16, name="u_psum")
-        nc.tensor.matmul(u_psum[:], down[:, C : C + Q], tokens[:], start=True, stop=True)
+        halves = [slice(h * HALF, (h + 1) * HALF) for h in range(2)]
+
+        u_psum = [psum.tile([Q, HALF], BF16, name="u_psum%d" % h) for h in range(2)]
+        for h in range(2):
+            nc.tensor.matmul(u_psum[h][:], down[:, C : C + Q], tokens[:, halves[h]], start=True, stop=True)
         y_psum = psum.tile([C, N], F32, name="y_psum")
         nc.tensor.matmul(y_psum[:], down[:, 0:C], tokens[:], start=True, stop=True)
 
-        u_own = held.tile([Q, N], BF16, name="u_own")
-        nc.vector.tensor_tensor(u_own[:], u_psum[:], own[:], mybir.AluOpType.mult)
-
-        d_psum = psum.tile([C, N], F32, name="d_psum")
-        nc.tensor.matmul(d_psum[:], up[:], u_own[:], start=True, stop=True)
+        u_own = [held.tile([Q, HALF], BF16, name="u_own%d" % h) for h in range(2)]
+        d_psum = [psum.tile([C, HALF], F32, name="d_psum%d" % h) for h in range(2)]
+        for h in range(2):
+            nc.vector.tensor_tensor(u_own[h][:], u_psum[h][:], own[:, halves[h]], mybir.AluOpType.mult)
+            nc.tensor.matmul(d_psum[h][:], up[:], u_own[h][:], start=True, stop=True)
 
         y = held.tile([C, N], F32, name="y")
         nc.vector.tensor_copy(y[:], y_psum[:])
         d = held.tile([C, N], F32, name="d")
-        nc.vector.tensor_copy(d[:], d_psum[:])
+        for h in range(2):
+            nc.vector.tensor_copy(d[:, halves[h]], d_psum[h][:])
 
         nc.vector.tensor_tensor(cache[:].indirect(offsets[:]), y[:], d[:], mybir.AluOpType.add)
 

@@ -25,30 +25,33 @@ def tile_llamaattentionwithlora_s_kernel(tc, base, x, wka, wb, offs, out):
         nc.scalar.dma_start(down[:], wka)
         offsets = held.tile([C, N // 16], U16, name="offsets")
         nc.sync.dma_start(offsets[:], offs)
-        up = held.tile([Q, C], BF16, name="up")
-        nc.scalar.dma_start(up[:], wb)
+        up = held.tile([RANK, ADAPTERS, C], BF16, name="up")
+        nc.scalar.dma_start(up[:], wb.rearrange("(a r) c -> r a c", r=RANK))
         cache = held.tile([C, S], F32, name="cache")
         nc.sync.dma_start(cache[:], base)
 
-        own = held.tile([Q, N], BF16, name="own")
-        nc.vector.memset(own[:], 0.0)
-        for a in range(ADAPTERS):
-            block = slice(a * RANK, (a + 1) * RANK)
-            nc.vector.memset(own[block, block], 1.0)
-
         halves = [slice(h * HALF, (h + 1) * HALF) for h in range(2)]
 
-        u_psum = [psum.tile([Q, HALF], BF16, name="u_psum%d" % h) for h in range(2)]
-        for h in range(2):
-            nc.tensor.matmul(u_psum[h][:], down[:, C : C + Q], tokens[:, halves[h]], start=True, stop=True)
+        u_psum = [psum.tile([RANK, HALF], BF16, name="u_psum%d" % h) for h in range(2)]
+        for a in range(ADAPTERS):
+            h, place = a // 2, slice((a % 2) * RANK, (a % 2 + 1) * RANK)
+            nc.tensor.matmul(
+                u_psum[h][:, place],
+                down[:, C + a * RANK : C + (a + 1) * RANK],
+                tokens[:, a * RANK : (a + 1) * RANK],
+                start=True,
+                stop=True,
+            )
         y_psum = psum.tile([C, N], F32, name="y_psum")
         nc.tensor.matmul(y_psum[:], down[:, 0:C], tokens[:], start=True, stop=True)
 
-        u_own = [held.tile([Q, HALF], BF16, name="u_own%d" % h) for h in range(2)]
+        u_own = [held.tile([RANK, HALF], BF16, name="u_own%d" % h) for h in range(2)]
         d_psum = [psum.tile([C, HALF], F32, name="d_psum%d" % h) for h in range(2)]
         for h in range(2):
-            nc.vector.tensor_tensor(u_own[h][:], u_psum[h][:], own[:, halves[h]], mybir.AluOpType.mult)
-            nc.tensor.matmul(d_psum[h][:], up[:], u_own[h][:], start=True, stop=True)
+            nc.vector.tensor_copy(u_own[h][:], u_psum[h][:])
+            for a in (2 * h, 2 * h + 1):
+                place = slice((a % 2) * RANK, (a % 2 + 1) * RANK)
+                nc.tensor.matmul(d_psum[h][:, place], up[:, a, :], u_own[h][:, place], start=True, stop=True)
 
         y = held.tile([C, N], F32, name="y")
         nc.vector.tensor_copy(y[:], y_psum[:])

@@ -19,10 +19,10 @@ def tile_llamaattentionwithlora_s_kernel(tc, base, x, wka, wb, offs, out):
         tc.tile_pool(name="held", bufs=1) as held,
         tc.psum_pool(name="psum", bufs=1) as psum,
     ):
-        tokens = held.tile([C, N], BF16, name="tokens")
-        nc.sync.dma_start(tokens[:], x)
         down = held.tile([C, C + Q], BF16, name="down")
-        nc.scalar.dma_start(down[:], wka)
+        nc.sync.dma_start(down[:], wka)
+        tokens = held.tile([C, N], BF16, name="tokens")
+        nc.scalar.dma_start(tokens[:], x)
         offsets = held.tile([C, N // 16], U16, name="offsets")
         nc.sync.dma_start(offsets[:], offs)
         up = held.tile([RANK, ADAPTERS, C], BF16, name="up")

@@ -23,12 +23,12 @@ def tile_llamaattentionwithlora_s_kernel(tc, base, x, wka, wb, offs, out):
         nc.sync.dma_start(down[:], wka)
         tokens = held.tile([C, N], BF16, name="tokens")
         nc.scalar.dma_start(tokens[:], x)
+        up = held.tile([RANK, ADAPTERS, C], BF16, name="up")
+        nc.sync.dma_start(up[:], wb.rearrange("(a r) c -> r a c", r=RANK))
         offsets = held.tile([C, N // 16], U16, name="offsets")
         nc.sync.dma_start(offsets[:], offs)
-        up = held.tile([RANK, ADAPTERS, C], BF16, name="up")
-        nc.scalar.dma_start(up[:], wb.rearrange("(a r) c -> r a c", r=RANK))
         cache = held.tile([C, S], F32, name="cache")
-        nc.sync.dma_start(cache[:], base)
+        nc.scalar.dma_start(cache[:], base)
 
         halves = [slice(h * HALF, (h + 1) * HALF) for h in range(2)]
 

@@ -19,12 +19,14 @@ def tile_llamaattentionwithlora_s_kernel(tc, base, x, wka, wb, offs, out):
         tc.tile_pool(name="held", bufs=1) as held,
         tc.psum_pool(name="psum", bufs=1) as psum,
     ):
-        down = held.tile([C, C + Q], BF16, name="down")
-        nc.sync.dma_start(down[:], wka)
+        down = held.tile([C, Q], BF16, name="down")
+        nc.sync.dma_start(down[:], wka[:, C : C + Q])
         tokens = held.tile([C, N], BF16, name="tokens")
         nc.scalar.dma_start(tokens[:], x)
+        key = held.tile([C, C], BF16, name="key")
+        nc.sync.dma_start(key[:], wka[:, 0:C])
         up = held.tile([RANK, ADAPTERS, C], BF16, name="up")
-        nc.sync.dma_start(up[:], wb.rearrange("(a r) c -> r a c", r=RANK))
+        nc.scalar.dma_start(up[:], wb.rearrange("(a r) c -> r a c", r=RANK))
         offsets = held.tile([C, N // 16], U16, name="offsets")
         nc.sync.dma_start(offsets[:], offs)
         cache = held.tile([C, S], F32, name="cache")
@@ -37,13 +39,13 @@ def tile_llamaattentionwithlora_s_kernel(tc, base, x, wka, wb, offs, out):
             h, place = a // 2, slice((a % 2) * RANK, (a % 2 + 1) * RANK)
             nc.tensor.matmul(
                 u_psum[h][:, place],
-                down[:, C + a * RANK : C + (a + 1) * RANK],
+                down[:, a * RANK : (a + 1) * RANK],
                 tokens[:, a * RANK : (a + 1) * RANK],
                 start=True,
                 stop=True,
             )
         y_psum = psum.tile([C, N], F32, name="y_psum")
-        nc.tensor.matmul(y_psum[:], down[:, 0:C], tokens[:], start=True, stop=True)
+        nc.tensor.matmul(y_psum[:], key[:], tokens[:], start=True, stop=True)
 
         u_own = [held.tile([RANK, HALF], BF16, name="u_own%d" % h) for h in range(2)]
         d_psum = [psum.tile([C, HALF], F32, name="d_psum%d" % h) for h in range(2)]

@@ -25,35 +25,31 @@ def tile_llamaattentionwithlora_s_kernel(tc, base, x, wka, wb, offs, out):
         nc.scalar.dma_start(tokens[:], x)
         key = held.tile([C, C], BF16, name="key")
         nc.sync.dma_start(key[:], wka[:, 0:C])
-        up = held.tile([RANK, ADAPTERS, C], BF16, name="up")
-        nc.scalar.dma_start(up[:], wb.rearrange("(a r) c -> r a c", r=RANK))
+        up = held.tile([Q, C], BF16, name="up")
+        nc.scalar.dma_start(up[:], wb)
         offsets = held.tile([C, N // 16], U16, name="offsets")
         nc.sync.dma_start(offsets[:], offs)
         cache = held.tile([C, S], F32, name="cache")
         nc.scalar.dma_start(cache[:], base)
 
-        halves = [slice(h * HALF, (h + 1) * HALF) for h in range(2)]
-
-        u_psum = [psum.tile([RANK, HALF], BF16, name="u_psum%d" % h) for h in range(2)]
+        zeros = held.tile([C, N], BF16, name="zeros")
+        nc.vector.memset(zeros[:], 0.0)
+        u_psum = psum.tile([Q, N], BF16, name="u_psum")
+        nc.tensor.matmul(u_psum[:], zeros[:], zeros[:], start=True, stop=True)
         for a in range(ADAPTERS):
-            h, place = a // 2, slice((a % 2) * RANK, (a % 2 + 1) * RANK)
+            own = slice(a * RANK, (a + 1) * RANK)
             nc.tensor.matmul(
-                u_psum[h][:, place],
-                down[:, a * RANK : (a + 1) * RANK],
-                tokens[:, a * RANK : (a + 1) * RANK],
-                start=True,
-                stop=True,
+                u_psum[own, own], down[:, own], tokens[:, own], start=True, stop=True
             )
         y_psum = psum.tile([C, N], F32, name="y_psum")
         nc.tensor.matmul(y_psum[:], key[:], tokens[:], start=True, stop=True)
 
-        u_own = [held.tile([RANK, HALF], BF16, name="u_own%d" % h) for h in range(2)]
+        halves = [slice(h * HALF, (h + 1) * HALF) for h in range(2)]
+        u_own = [held.tile([Q, HALF], BF16, name="u_own%d" % h) for h in range(2)]
         d_psum = [psum.tile([C, HALF], F32, name="d_psum%d" % h) for h in range(2)]
         for h in range(2):
-            nc.vector.tensor_copy(u_own[h][:], u_psum[h][:])
-            for a in (2 * h, 2 * h + 1):
-                place = slice((a % 2) * RANK, (a % 2 + 1) * RANK)
-                nc.tensor.matmul(d_psum[h][:, place], up[:, a, :], u_own[h][:, place], start=True, stop=True)
+            nc.vector.tensor_copy(u_own[h][:], u_psum[:, halves[h]])
+            nc.tensor.matmul(d_psum[h][:], up[:], u_own[h][:], start=True, stop=True)
 
         y = held.tile([C, N], F32, name="y")
         nc.vector.tensor_copy(y[:], y_psum[:])

import concourse.mybir as mybir

BF16, F32, U16 = mybir.dt.bfloat16, mybir.dt.float32, mybir.dt.uint16

C = 128
S = 512
N = 128
RANK = 32
ADAPTERS = 4
Q = ADAPTERS * RANK
HALF = N // 2

FLOPS = 2 * C * C * N + 2 * C * Q * N + 2 * RANK * C * N


def tile_llamaattentionwithlora_s_kernel(tc, base, x, wka, wb, offs, out):
    nc = tc.nc
    with (
        tc.tile_pool(name="held", bufs=1) as held,
        tc.psum_pool(name="psum", bufs=1) as psum,
    ):
        down = held.tile([C, Q], BF16, name="down")
        nc.sync.dma_start(down[:], wka[:, C : C + Q])
        tokens = held.tile([C, N], BF16, name="tokens")
        nc.scalar.dma_start(tokens[:], x)
        key = held.tile([C, C], BF16, name="key")
        nc.sync.dma_start(key[:], wka[:, 0:C])
        up = held.tile([Q, C], BF16, name="up")
        nc.scalar.dma_start(up[:], wb)
        offsets = held.tile([C, N // 16], U16, name="offsets")
        nc.sync.dma_start(offsets[:], offs)
        cache = held.tile([C, S], F32, name="cache")
        nc.scalar.dma_start(cache[:], base)

        zeros = held.tile([C, N], BF16, name="zeros")
        nc.vector.memset(zeros[:], 0.0)
        u_psum = psum.tile([Q, N], BF16, name="u_psum")
        nc.tensor.matmul(u_psum[:], zeros[:], zeros[:], start=True, stop=True)
        for a in range(ADAPTERS):
            own = slice(a * RANK, (a + 1) * RANK)
            nc.tensor.matmul(
                u_psum[own, own], down[:, own], tokens[:, own], start=True, stop=True
            )
        y_psum = psum.tile([C, N], F32, name="y_psum")
        nc.tensor.matmul(y_psum[:], key[:], tokens[:], start=True, stop=True)

        halves = [slice(h * HALF, (h + 1) * HALF) for h in range(2)]
        u_own = [held.tile([Q, HALF], BF16, name="u_own%d" % h) for h in range(2)]
        d_psum = [psum.tile([C, HALF], F32, name="d_psum%d" % h) for h in range(2)]
        for h in range(2):
            nc.vector.tensor_copy(u_own[h][:], u_psum[:, halves[h]])
            nc.tensor.matmul(d_psum[h][:], up[:], u_own[h][:], start=True, stop=True)

        y = held.tile([C, N], F32, name="y")
        nc.vector.tensor_copy(y[:], y_psum[:])
        d = held.tile([C, N], F32, name="d")
        for h in range(2):
            nc.vector.tensor_copy(d[:, halves[h]], d_psum[h][:])

        nc.vector.tensor_tensor(cache[:].indirect(offsets[:]), y[:], d[:], mybir.AluOpType.add)

        nc.sync.dma_start(out, cache[:])
